import numpy as np
import ml_dtypes

BF16 = ml_dtypes.bfloat16


def bf(x):
    return np.asarray(x, np.float32).astype(BF16)


def f32(x):
    return np.asarray(x, np.float32)


def f64(x):
    return np.asarray(x).astype(np.float64)


def striped(idx):
    return np.tile(idx.reshape(-1, 16).T, (8, 1))


S, D, F, A, N, R = 2048, 128, 128, 512, 8192, 1024
NEG_SLOPE = 0.01


def setup_inputs():
    table = bf(np.random.standard_normal((S, D)))
    w = bf(np.random.standard_normal((D, F)) / np.sqrt(D))
    b = f32(0.1 * np.random.standard_normal((F, 1)))
    self_dst = bf(np.random.standard_normal((F, N)))
    attn_w = bf(np.random.standard_normal((F + F, A)) / np.sqrt(F + F))
    attn_b = f32(0.1 * np.random.standard_normal((A, 1)))
    idx = np.concatenate([np.random.permutation(S)[:R] for _ in range(N // R)])
    return {"table": table, "w": w, "b": b, "self_dst": self_dst, "attn_w": attn_w, "attn_b": attn_b, "offs": striped(idx)}


def reference(table, w, b, self_dst, attn_w, attn_b, offs):
    idx = offs[:16].T.reshape(-1)
    z = f64(w).T @ f64(table)[idx].T + f64(b)
    u = f64(attn_w)[:F].T @ z + f64(attn_w)[F:].T @ f64(self_dst) + f64(attn_b)
    e = np.where(u >= 0, u, NEG_SLOPE * u)
    return np.concatenate([z, e], axis=0)

@@ -1,0 +1,107 @@
+import concourse.mybir as mybir
+from concourse.masks import make_identity
+
+BF16, F32, U16 = mybir.dt.bfloat16, mybir.dt.float32, mybir.dt.uint16
+ADD, MULT, MAX = mybir.AluOpType.add, mybir.AluOpType.mult, mybir.AluOpType.max
+IDENTITY = mybir.ActivationFunctionType.Identity
+
+P = 128
+NODES = 2048
+HEADS = 512
+EDGES = 8192
+PIECE = 512
+STORE = 2048
+NEG_SLOPE = 0.01
+
+FLOPS = 2 * P * P * EDGES + 2 * (2 * P) * HEADS * EDGES
+
+
+def tile_reledgeupdate_b_kernel(tc, table, w, b, self_dst, attn_w, attn_b, offs, out):
+    nc = tc.nc
+    with (
+        tc.tile_pool(name="held", bufs=1) as held,
+        tc.tile_pool(name="scaled", bufs=4) as scaled,
+        tc.tile_pool(name="staged", bufs=4) as staged,
+        tc.psum_pool(name="banks", bufs=8) as banks,
+    ):
+        offsets = held.tile([P, EDGES // 16], U16, name="offsets")
+        nc.sync.dma_start(offsets[:], offs)
+
+        rows = held.tile([P, NODES // P, P], BF16, name="rows")
+        nc.scalar.dma_start(rows[:], table.rearrange("(a p) d -> p a d", p=P))
+        w_sb = held.tile([P, P], BF16, name="w_sb")
+        nc.scalar.dma_start(w_sb[:], w)
+
+        identity = held.tile([P, P], BF16, name="identity")
+        make_identity(nc, identity[:])
+
+        b_sb = held.tile([P, 1], F32, name="b_sb")
+        attn_b_sb = held.tile([P, HEADS // P], F32, name="attn_b_sb")
+        with nc.allow_non_contiguous_dma(reason="one bias value to a partition"):
+            nc.gpsimd.dma_start(b_sb[:], b)
+            nc.gpsimd.dma_start(attn_b_sb[:], attn_b.rearrange("(a p) o -> p (a o)", p=P))
+        attn_sb = held.tile([P, 2, HEADS], BF16, name="attn_sb")
+        nc.gpsimd.dma_start(attn_sb[:], attn_w.rearrange("(k f) h -> f k h", f=P))
+        dst_sb = held.tile([P, EDGES], BF16, name="dst_sb")
+        nc.gpsimd.dma_start(dst_sb[:], self_dst)
+
+        attn_b_low = held.tile([P, HEADS // P], F32, name="attn_b_low")
+        nc.vector.tensor_scalar_mul(attn_b_low[:], attn_b_sb[:], NEG_SLOPE)
+
+        window = held.tile([P, NODES], BF16, name="window")
+        half = NODES // 2
+        for side in range(2):
+            flipped = banks.tile([P, half], BF16, tag="bank")
+            for k in range(half // P):
+                nc.tensor.transpose(
+                    flipped[:, k * P : (k + 1) * P], rows[:, side * (half // P) + k, :], identity[:]
+                )
+            if side == 0:
+                nc.vector.tensor_copy(window[:, 0:half], flipped[:])
+            else:
+                nc.scalar.copy(window[:, half:NODES], flipped[:])
+
+        z_bf = held.tile([P, EDGES], BF16, name="z_bf")
+        for g in range(EDGES // STORE):
+            z_out = staged.tile([P, STORE], F32, tag="staged")
+            for c in range(STORE // PIECE):
+                j = g * (STORE // PIECE) + c
+                z_ps = banks.tile([P, PIECE], F32, tag="bank")
+                nc.tensor.matmul(
+                    z_ps[:],
+                    w_sb[:],
+                    window[:].indirect(offsets[:, j * (PIECE // 16) : (j + 1) * (PIECE // 16)]),
+                    start=True,
+                    stop=True,
+                )
+                nc.scalar.activation(
+                    z_out[:, c * PIECE : (c + 1) * PIECE], z_ps[:], IDENTITY, bias=b_sb[:, 0:1], scale=1.0
+                )
+                nc.vector.tensor_scalar_add(z_bf[:, j * PIECE : (j + 1) * PIECE], z_ps[:], b_sb[:, 0:1])
+            nc.sync.dma_start(out[0:P, g * STORE : (g + 1) * STORE], z_out[:])
+
+        for g in range(EDGES // STORE):
+            for h in range(HEADS // P):
+                e_out = staged.tile([P, STORE], F32, tag="staged")
+                for c in range(STORE // PIECE):
+                    j = g * (STORE // PIECE) + c
+                    u_ps = banks.tile([P, PIECE], F32, tag="bank")
+                    nc.tensor.matmul(
+                        u_ps[:], attn_sb[:, 0, h * P : (h + 1) * P], z_bf[:, j * PIECE : (j + 1) * PIECE],
+                        start=True, stop=False,
+                    )
+                    nc.tensor.matmul(
+                        u_ps[:], attn_sb[:, 1, h * P : (h + 1) * P], dst_sb[:, j * PIECE : (j + 1) * PIECE],
+                        start=False, stop=True,
+                    )
+                    low = scaled.tile([P, PIECE], F32, tag="low")
+                    nc.scalar.activation(
+                        low[:], u_ps[:], IDENTITY, bias=attn_b_low[:, h : h + 1], scale=NEG_SLOPE
+                    )
+                    nc.vector.scalar_tensor_tensor(
+                        e_out[:, c * PIECE : (c + 1) * PIECE], u_ps[:], attn_b_sb[:, h : h + 1], low[:],
+                        op0=ADD, op1=MAX,
+                    )
+                nc.sync.dma_start(
+                    out[P + h * P : P + (h + 1) * P, g * STORE : (g + 1) * STORE], e_out[:]
+                )

@@ -2,7 +2,7 @@ import concourse.mybir as mybir
 from concourse.masks import make_identity
 
 BF16, F32, U16 = mybir.dt.bfloat16, mybir.dt.float32, mybir.dt.uint16
-ADD, MULT, MAX = mybir.AluOpType.add, mybir.AluOpType.mult, mybir.AluOpType.max
+MULT, MAX = mybir.AluOpType.mult, mybir.AluOpType.max
 IDENTITY = mybir.ActivationFunctionType.Identity
 
 P = 128
@@ -11,6 +11,7 @@ HEADS = 512
 EDGES = 8192
 PIECE = 512
 STORE = 2048
+CHUNK = 512
 NEG_SLOPE = 0.01
 
 FLOPS = 2 * P * P * EDGES + 2 * (2 * P) * HEADS * EDGES
@@ -20,46 +21,43 @@ def tile_reledgeupdate_b_kernel(tc, table, w, b, self_dst, attn_w, attn_b, offs,
     nc = tc.nc
     with (
         tc.tile_pool(name="held", bufs=1) as held,
-        tc.tile_pool(name="scaled", bufs=4) as scaled,
         tc.tile_pool(name="staged", bufs=4) as staged,
         tc.psum_pool(name="banks", bufs=8) as banks,
     ):
-        offsets = held.tile([P, EDGES // 16], U16, name="offsets")
-        nc.sync.dma_start(offsets[:], offs)
-
-        rows = held.tile([P, NODES // P, P], BF16, name="rows")
-        nc.scalar.dma_start(rows[:], table.rearrange("(a p) d -> p a d", p=P))
-        w_sb = held.tile([P, P], BF16, name="w_sb")
-        nc.scalar.dma_start(w_sb[:], w)
-
+        per_row = CHUNK // P
+        raw = [held.tile([P, per_row, P], BF16, name=f"raw{k}") for k in range(NODES // CHUNK)]
+        for k in range(NODES // CHUNK):
+            nc.sync.dma_start(
+                raw[k][:], table[k * CHUNK : (k + 1) * CHUNK, :].rearrange("(p a) d -> p a d", a=per_row)
+            )
         identity = held.tile([P, P], BF16, name="identity")
         make_identity(nc, identity[:])
 
+        offsets = held.tile([P, EDGES // 16], U16, name="offsets")
+        nc.sync.dma_start(offsets[:], offs)
+        w_sb = held.tile([P, P], BF16, name="w_sb")
+        nc.sync.dma_start(w_sb[:], w)
         b_sb = held.tile([P, 1], F32, name="b_sb")
         attn_b_sb = held.tile([P, HEADS // P], F32, name="attn_b_sb")
         with nc.allow_non_contiguous_dma(reason="one bias value to a partition"):
-            nc.gpsimd.dma_start(b_sb[:], b)
-            nc.gpsimd.dma_start(attn_b_sb[:], attn_b.rearrange("(a p) o -> p (a o)", p=P))
+            nc.sync.dma_start(b_sb[:], b)
+            nc.sync.dma_start(attn_b_sb[:], attn_b.rearrange("(a p) o -> p (a o)", p=P))
         attn_sb = held.tile([P, 2, HEADS], BF16, name="attn_sb")
-        nc.gpsimd.dma_start(attn_sb[:], attn_w.rearrange("(k f) h -> f k h", f=P))
+        nc.sync.dma_start(attn_sb[:], attn_w.rearrange("(k f) h -> f k h", f=P))
         dst_sb = held.tile([P, EDGES], BF16, name="dst_sb")
-        nc.gpsimd.dma_start(dst_sb[:], self_dst)
-
-        attn_b_low = held.tile([P, HEADS // P], F32, name="attn_b_low")
-        nc.vector.tensor_scalar_mul(attn_b_low[:], attn_b_sb[:], NEG_SLOPE)
+        nc.sync.dma_start(dst_sb[:], self_dst)
 
         window = held.tile([P, NODES], BF16, name="window")
-        half = NODES // 2
-        for side in range(2):
-            flipped = banks.tile([P, half], BF16, tag="bank")
-            for k in range(half // P):
-                nc.tensor.transpose(
-                    flipped[:, k * P : (k + 1) * P], rows[:, side * (half // P) + k, :], identity[:]
-                )
-            if side == 0:
-                nc.vector.tensor_copy(window[:, 0:half], flipped[:])
+        for k in range(NODES // CHUNK):
+            flipped = banks.tile([P, PIECE], F32, tag="bank")
+            quarters = flipped[:].bitcast(BF16)[:, 0:CHUNK].rearrange("d (a p) -> d a p", a=per_row)
+            for a in range(per_row):
+                nc.tensor.transpose(quarters[:, a, :], raw[k][:, a, :], identity[:])
+            in_order = window[:, k * CHUNK : (k + 1) * CHUNK].rearrange("d (p a) -> d p a", a=per_row)
+            if k % 2 == 0:
+                nc.vector.tensor_copy(in_order, quarters.rearrange("d a p -> d p a"))
             else:
-                nc.scalar.copy(window[:, half:NODES], flipped[:])
+                nc.scalar.copy(in_order, quarters.rearrange("d a p -> d p a"))
 
         z_bf = held.tile([P, EDGES], BF16, name="z_bf")
         for g in range(EDGES // STORE):
@@ -74,15 +72,16 @@ def tile_reledgeupdate_b_kernel(tc, table, w, b, self_dst, attn_w, attn_b, offs,
                     start=True,
                     stop=True,
                 )
-                nc.scalar.activation(
-                    z_out[:, c * PIECE : (c + 1) * PIECE], z_ps[:], IDENTITY, bias=b_sb[:, 0:1], scale=1.0
-                )
-                nc.vector.tensor_scalar_add(z_bf[:, j * PIECE : (j + 1) * PIECE], z_ps[:], b_sb[:, 0:1])
+                z_piece = z_out[:, c * PIECE : (c + 1) * PIECE]
+                nc.scalar.activation(z_piece, z_ps[:], IDENTITY, bias=b_sb[:, 0:1], scale=1.0)
+                nc.vector.tensor_copy(z_bf[:, j * PIECE : (j + 1) * PIECE], z_piece)
             nc.sync.dma_start(out[0:P, g * STORE : (g + 1) * STORE], z_out[:])
 
         for g in range(EDGES // STORE):
             for h in range(HEADS // P):
                 e_out = staged.tile([P, STORE], F32, tag="staged")
+                e_rows = out[P + h * P : P + (h + 1) * P, :]
+                last_tile = g == EDGES // STORE - 1 and h == HEADS // P - 1
                 for c in range(STORE // PIECE):
                     j = g * (STORE // PIECE) + c
                     u_ps = banks.tile([P, PIECE], F32, tag="bank")
@@ -94,14 +93,10 @@ def tile_reledgeupdate_b_kernel(tc, table, w, b, self_dst, attn_w, attn_b, offs,
                         u_ps[:], attn_sb[:, 1, h * P : (h + 1) * P], dst_sb[:, j * PIECE : (j + 1) * PIECE],
                         start=False, stop=True,
                     )
-                    low = scaled.tile([P, PIECE], F32, tag="low")
-                    nc.scalar.activation(
-                        low[:], u_ps[:], IDENTITY, bias=attn_b_low[:, h : h + 1], scale=NEG_SLOPE
-                    )
-                    nc.vector.scalar_tensor_tensor(
-                        e_out[:, c * PIECE : (c + 1) * PIECE], u_ps[:], attn_b_sb[:, h : h + 1], low[:],
-                        op0=ADD, op1=MAX,
-                    )
-                nc.sync.dma_start(
-                    out[P + h * P : P + (h + 1) * P, g * STORE : (g + 1) * STORE], e_out[:]
-                )
+                    e_piece = e_out[:, c * PIECE : (c + 1) * PIECE]
+                    nc.scalar.activation(e_piece, u_ps[:], IDENTITY, bias=attn_b_sb[:, h : h + 1], scale=1.0)
+                    nc.vector.scalar_tensor_tensor(e_piece, e_piece, NEG_SLOPE, e_piece, op0=MULT, op1=MAX)
+                    if last_tile:
+                        nc.sync.dma_start(e_rows[:, j * PIECE : (j + 1) * PIECE], e_piece)
+                if not last_tile:
+                    nc.sync.dma_start(e_rows[:, g * STORE : (g + 1) * STORE], e_out[:])

import concourse.mybir as mybir
from concourse.masks import make_identity

BF16, F32, U16 = mybir.dt.bfloat16, mybir.dt.float32, mybir.dt.uint16
MULT, MAX = mybir.AluOpType.mult, mybir.AluOpType.max
IDENTITY = mybir.ActivationFunctionType.Identity

P = 128
NODES = 2048
HEADS = 512
EDGES = 8192
PIECE = 512
STORE = 2048
CHUNK = 512
NEG_SLOPE = 0.01

FLOPS = 2 * P * P * EDGES + 2 * (2 * P) * HEADS * EDGES


def tile_reledgeupdate_b_kernel(tc, table, w, b, self_dst, attn_w, attn_b, offs, out):
    nc = tc.nc
    with (
        tc.tile_pool(name="held", bufs=1) as held,
        tc.tile_pool(name="staged", bufs=4) as staged,
        tc.psum_pool(name="banks", bufs=8) as banks,
    ):
        per_row = CHUNK // P
        raw = [held.tile([P, per_row, P], BF16, name=f"raw{k}") for k in range(NODES // CHUNK)]
        for k in range(NODES // CHUNK):
            nc.sync.dma_start(
                raw[k][:], table[k * CHUNK : (k + 1) * CHUNK, :].rearrange("(p a) d -> p a d", a=per_row)
            )
        identity = held.tile([P, P], BF16, name="identity")
        make_identity(nc, identity[:])

        offsets = held.tile([P, EDGES // 16], U16, name="offsets")
        nc.sync.dma_start(offsets[:], offs)
        w_sb = held.tile([P, P], BF16, name="w_sb")
        nc.sync.dma_start(w_sb[:], w)
        b_sb = held.tile([P, 1], F32, name="b_sb")
        attn_b_sb = held.tile([P, HEADS // P], F32, name="attn_b_sb")
        with nc.allow_non_contiguous_dma(reason="one bias value to a partition"):
            nc.sync.dma_start(b_sb[:], b)
            nc.sync.dma_start(attn_b_sb[:], attn_b.rearrange("(a p) o -> p (a o)", p=P))
        attn_sb = held.tile([P, 2, HEADS], BF16, name="attn_sb")
        nc.sync.dma_start(attn_sb[:], attn_w.rearrange("(k f) h -> f k h", f=P))
        dst_sb = held.tile([P, EDGES], BF16, name="dst_sb")
        nc.sync.dma_start(dst_sb[:], self_dst)

        window = held.tile([P, NODES], BF16, name="window")
        for k in range(NODES // CHUNK):
            flipped = banks.tile([P, PIECE], F32, tag="bank")
            quarters = flipped[:].bitcast(BF16)[:, 0:CHUNK].rearrange("d (a p) -> d a p", a=per_row)
            for a in range(per_row):
                nc.tensor.transpose(quarters[:, a, :], raw[k][:, a, :], identity[:])
            in_order = window[:, k * CHUNK : (k + 1) * CHUNK].rearrange("d (p a) -> d p a", a=per_row)
            if k % 2 == 0:
                nc.vector.tensor_copy(in_order, quarters.rearrange("d a p -> d p a"))
            else:
                nc.scalar.copy(in_order, quarters.rearrange("d a p -> d p a"))

        z_bf = held.tile([P, EDGES], BF16, name="z_bf")
        for g in range(EDGES // STORE):
            z_out = staged.tile([P, STORE], F32, tag="staged")
            for c in range(STORE // PIECE):
                j = g * (STORE // PIECE) + c
                z_ps = banks.tile([P, PIECE], F32, tag="bank")
                nc.tensor.matmul(
                    z_ps[:],
                    w_sb[:],
                    window[:].indirect(offsets[:, j * (PIECE // 16) : (j + 1) * (PIECE // 16)]),
                    start=True,
                    stop=True,
                )
                z_piece = z_out[:, c * PIECE : (c + 1) * PIECE]
                nc.scalar.activation(z_piece, z_ps[:], IDENTITY, bias=b_sb[:, 0:1], scale=1.0)
                nc.vector.tensor_copy(z_bf[:, j * PIECE : (j + 1) * PIECE], z_piece)
            nc.sync.dma_start(out[0:P, g * STORE : (g + 1) * STORE], z_out[:])

        for g in range(EDGES // STORE):
            for h in range(HEADS // P):
                e_out = staged.tile([P, STORE], F32, tag="staged")
                e_rows = out[P + h * P : P + (h + 1) * P, :]
                last_tile = g == EDGES // STORE - 1 and h == HEADS // P - 1
                for c in range(STORE // PIECE):
                    j = g * (STORE // PIECE) + c
                    u_ps = banks.tile([P, PIECE], F32, tag="bank")
                    nc.tensor.matmul(
                        u_ps[:], attn_sb[:, 0, h * P : (h + 1) * P], z_bf[:, j * PIECE : (j + 1) * PIECE],
                        start=True, stop=False,
                    )
                    nc.tensor.matmul(
                        u_ps[:], attn_sb[:, 1, h * P : (h + 1) * P], dst_sb[:, j * PIECE : (j + 1) * PIECE],
                        start=False, stop=True,
                    )
                    e_piece = e_out[:, c * PIECE : (c + 1) * PIECE]
                    nc.scalar.activation(e_piece, u_ps[:], IDENTITY, bias=attn_b_sb[:, h : h + 1], scale=1.0)
                    nc.vector.scalar_tensor_tensor(e_piece, e_piece, NEG_SLOPE, e_piece, op0=MULT, op1=MAX)
                    if last_tile:
                        nc.sync.dma_start(e_rows[:, j * PIECE : (j + 1) * PIECE], e_piece)
                if not last_tile:
                    nc.sync.dma_start(e_rows[:, g * STORE : (g + 1) * STORE], e_out[:])
